import numpy as np
import ml_dtypes


def mxq(x, axis, fmt="e4m3"):
    dtype, down = {"e4m3": (ml_dtypes.float8_e4m3fn, 7), "e5m2": (ml_dtypes.float8_e5m2, 14)}[fmt]
    v = np.moveaxis(np.asarray(x, np.float32).astype(ml_dtypes.bfloat16).astype(np.float64), axis, -1)
    blocks = v.reshape(v.shape[:-1] + (-1, 32))
    amax = np.abs(blocks).max(-1, keepdims=True)
    byte = np.maximum(np.where(amax > 0, np.frexp(amax)[1] - 1 + 127, 0) - down, 1)
    scale = np.exp2(byte - 127.0)
    codes = (blocks / scale).astype(np.float32).astype(dtype).astype(np.float64)
    return np.moveaxis((codes * scale).reshape(v.shape), -1, axis)


WIDE = False


def mx_kscale(k):
    if not WIDE:
        return np.ones(k)
    levels = np.array([10, -10, 5, -5, 0])
    a = np.random.permutation(np.resize(levels, k // 512 * 4)).reshape(k // 512, 4)
    idx = np.arange(k)
    return np.exp2(a[idx // 512, idx % 128 // 32])


BF16 = ml_dtypes.bfloat16


def bf(x):
    return np.asarray(x, np.float32).astype(BF16)


def f64(x):
    return np.asarray(x).astype(np.float64)


N, DIN, DHID, DOUT, DMLP, NF = 256, 1024, 2048, 512, 512, 8
G = 3 * DHID
FS = N // NF
SYNC = 0.15


def sigmoid(v):
    return 1.0 / (1.0 + np.exp(-v))


def setup_inputs():
    s = mx_kscale(DOUT)
    o = np.random.standard_normal((N, DOUT)) * (0.8 + 0.8 * np.random.random((N, 1)))
    rows = np.concatenate([0.55 / np.sqrt(DOUT) / s, np.array([0.3])])
    return {
        "eng_out": bf(o * s),
        "tension": bf((o * o).mean(-1)),
        "hiddens": bf(np.random.standard_normal((N, DHID)) * (0.5 + np.random.random((N, 1)))),
        "w_ih": bf(np.random.standard_normal((DOUT + 1, G)) * rows[:, None]),
        "b_ih": bf(np.random.standard_normal(G) * 0.3),
        "w_hh": bf(np.random.standard_normal((DHID, G)) * 0.7 / np.sqrt(DHID)),
        "b_hh": bf(np.random.standard_normal(G) * 0.3),
    }


def reference(eng_out, tension, hiddens, w_ih, b_ih, w_hh, b_hh):
    h = f64(hiddens)
    wi = f64(w_ih)
    gi = (mxq(f64(eng_out), 1, "e4m3") @ mxq(wi[:DOUT], 0, "e4m3")) + f64(tension)[:, None] * wi[DOUT] + f64(b_ih)
    gh = (mxq(h, 1, "e4m3") @ mxq(f64(w_hh), 0, "e4m3")) + f64(b_hh)
    ir, iz, inn = np.split(gi, 3, axis=-1)
    hr, hz, hn = np.split(gh, 3, axis=-1)
    r = sigmoid(ir + hr)
    z = sigmoid(iz + hz)
    ncand = np.tanh(inn + r * hn)
    h_new = (1.0 - z) * ncand + z * h
    hf = h_new.reshape(NF, FS, DHID)
    fmean = hf.mean(axis=1, keepdims=True)
    hf = (1.0 - SYNC) * hf + SYNC * fmean
    return hf.reshape(N, DHID)

@@ -1,0 +1,227 @@
+from contextlib import ExitStack
+
+import concourse.mybir as mybir
+from concourse.masks import make_identity
+
+FP8X4 = mybir.dt.float8_e4m3fn_x4
+BF16 = mybir.dt.bfloat16
+F32 = mybir.dt.float32
+U32 = mybir.dt.uint32
+U8 = mybir.dt.uint8
+I32 = mybir.dt.int32
+ALU = mybir.AluOpType
+ACT = mybir.ActivationFunctionType
+
+P = 128
+CELLS = 256
+DOUT = 512
+DHID = 2048
+K_PASS = 512
+PASSES = 5
+GATES = 3
+UNITS = PASSES * GATES
+SYNC = 0.15
+FACTION = 32
+
+FLOPS = 2 * CELLS * (DOUT + DHID) * GATES * DHID
+
+ROUNDS = ((0, 512), (512, 512), (1024, 512), (1536, 512))
+
+
+def tile_fractalengine_pb_kernel(tc, eng_out, tension, hiddens, w_ih, b_ih, w_hh, b_hh, out):
+    nc = tc.nc
+    with ExitStack() as ctx:
+        const = ctx.enter_context(tc.tile_pool(name="const", bufs=1))
+        rawp = ctx.enter_context(tc.tile_pool(name="rawp", bufs=8))
+        grp = ctx.enter_context(tc.tile_pool(name="grp", bufs=4))
+        cod = ctx.enter_context(tc.tile_pool(name="cod", bufs=2))
+        epi = ctx.enter_context(tc.tile_pool(name="epi", bufs=3))
+        outp = ctx.enter_context(tc.tile_pool(name="outp", bufs=2))
+        ps_a = ctx.enter_context(tc.psum_pool(name="ps_a", bufs=2))
+        ps_b = ctx.enter_context(tc.psum_pool(name="ps_b", bufs=1))
+
+        ident = const.tile([P, P], F32)
+        make_identity(nc, ident[:])
+        ident_bf = const.tile([P, P], BF16)
+        make_identity(nc, ident_bf[:])
+
+        vraw = const.tile([P, P], BF16)
+        nc.vector.memset(vraw[:].bitcast(I32), 0)
+        lift = const.tile([P, CELLS], BF16)
+        nc.vector.memset(lift[:].bitcast(I32), 0)
+        nc.vector.memset(lift[32:64, :], 1.0)
+        nc.vector.memset(lift[64:96, :], 1.0)
+        rows = const.tile([P, 2 * DHID], BF16)
+        nc.vector.memset(rows[:].bitcast(I32), 0)
+        tens = const.tile([P, CELLS], BF16)
+
+        last = w_ih[DOUT : DOUT + 1, :]
+        nc.scalar.dma_start(out=vraw[0:16, :], in_=last[:, 0:DHID].rearrange("o (r c) -> (o r) c", c=P))
+        nc.scalar.dma_start(out=vraw[16:32, :], in_=b_ih[0:DHID].rearrange("(r c) -> r c", c=P))
+        nc.scalar.dma_start(out=vraw[32:48, :], in_=b_hh[0:DHID].rearrange("(r c) -> r c", c=P))
+        nc.scalar.dma_start(out=vraw[48:64, :], in_=b_hh[2 * DHID : 3 * DHID].rearrange("(r c) -> r c", c=P))
+        nc.scalar.dma_start(out=tens[:], in_=tension.partition_broadcast(P))
+        nc.scalar.dma_start(out=lift[0:1, :], in_=tension.rearrange("(o n) -> o n", o=1))
+        nc.scalar.dma_start(out=rows[0:1, :], in_=last[:, DHID : 3 * DHID])
+        nc.scalar.dma_start(out=rows[32:33, :], in_=b_ih[DHID : 3 * DHID].rearrange("(o n) -> o n", o=1))
+        nc.scalar.dma_start(out=rows[64:65, 0:DHID], in_=b_hh[DHID : 2 * DHID].rearrange("(o n) -> o n", o=1))
+
+        vps = ps_b.tile([P, P], BF16, tag="spare")
+        nc.tensor.transpose(vps[:], vraw[:], ident_bf[:])
+        vec = const.tile([P, 64], F32)
+        nc.vector.tensor_copy(out=vec[:], in_=vps[:, 0:64])
+        bias_r = const.tile([P, 16], F32)
+        nc.vector.tensor_add(out=bias_r[:], in0=vec[:, 16:32], in1=vec[:, 32:48])
+
+        blocks = const.tile([P, P], F32)
+        nc.vector.memset(blocks[:], 0.0)
+        for f in range(P // FACTION):
+            span = slice(f * FACTION, (f + 1) * FACTION)
+            nc.vector.memset(blocks[span, span], 1.0)
+        diag = const.tile([P, P], F32)
+        nc.vector.tensor_scalar_mul(out=diag[:], in0=ident[:], scalar1=1.0 - SYNC)
+        mix = const.tile([P, P], F32)
+        nc.vector.scalar_tensor_tensor(
+            out=mix[:], in0=blocks[:], scalar=SYNC / FACTION, in1=diag[:], op0=ALU.mult, op1=ALU.add
+        )
+
+        h_nat = const.tile([P, 2, DHID], BF16)
+        e_nat = const.tile([P, 2, DOUT], BF16)
+        x_codes = const.tile([P, PASSES, CELLS], U32, align_bytes=64)
+        x_scales = const.tile([P, PASSES, CELLS], U8, align_bytes=64)
+
+        def load_x():
+            nc.sync.dma_start(out=e_nat[:], in_=eng_out.rearrange("(m p) k -> p m k", p=P))
+            nc.sync.dma_start(out=h_nat[:], in_=hiddens.rearrange("(m p) k -> p m k", p=P))
+
+        def prep_x(c):
+            words = (e_nat if c == 0 else h_nat)[:].bitcast(F32)
+            base = 0 if c == 0 else (c - 1) * (K_PASS // 2)
+            xt = ps_a.tile([P, 2, CELLS], F32, tag="bank_x" if c % 2 == 0 else "bank_y")
+            for u in range(2):
+                for m in range(2):
+                    nc.tensor.transpose(
+                        xt[:, u, m * P : (m + 1) * P],
+                        words[:, m, base + u : base + K_PASS // 2 : 2],
+                        ident[:],
+                    )
+            gx = grp.tile([P, CELLS, 4], BF16, align_bytes=64, tag="gx")
+            nc.vector.tensor_copy(out=gx[:].bitcast(F32), in_=xt[:].rearrange("p u n -> p n u"))
+            nc.vector.quantize_mx(
+                out=x_codes[:, c, :].bitcast(FP8X4),
+                scales=x_scales[:, c, :],
+                in_=gx[:].rearrange("p n t -> p (n t)"),
+            )
+
+        def quantise(codes, planes, g, u):
+            nc.vector.quantize_mx(
+                out=codes[:, u, :].bitcast(FP8X4),
+                scales=planes[:, u, :],
+                in_=g[:].rearrange("p w t -> p (w t)"),
+            )
+
+        def mx_group(acc, codes, planes, cols, gate, passes):
+            for c in passes:
+                u = c * GATES + gate
+                nc.tensor.matmul_mx(
+                    out=acc,
+                    lhsT=codes[:, u, cols].bitcast(FP8X4),
+                    lhsT_scale=planes[:, u, cols],
+                    rhs=x_codes[:, c, :].bitcast(FP8X4),
+                    rhs_scale=x_scales[:, c, :],
+                    start=(c == passes[0]),
+                    stop=(c == passes[-1]),
+                )
+
+        def flip_group(acc, row_cols, parts):
+            for m in range(2):
+                half = slice(m * P, (m + 1) * P)
+                nc.tensor.matmul(out=acc[:, half], lhsT=lift[:, half], rhs=rows[:, row_cols], start=True, stop=False)
+                for i, part in enumerate(parts):
+                    nc.tensor.matmul(
+                        out=acc[:, half],
+                        lhsT=part[:, half],
+                        rhs=ident[:],
+                        is_transpose=True,
+                        start=False,
+                        stop=(i == len(parts) - 1),
+                    )
+
+        for rnd, (d0, width) in enumerate(ROUNDS):
+            codes = cod.tile([P, UNITS, width], U32, align_bytes=64, tag="codes")
+            planes = cod.tile([P, UNITS, width], U8, align_bytes=64, tag="planes")
+            grouped = []
+
+            for c in range(PASSES):
+                for gate in range(GATES):
+                    u = c * GATES + gate
+                    cols = slice(gate * DHID + d0, gate * DHID + d0 + width)
+                    src = w_ih[0:K_PASS, cols] if c == 0 else w_hh[(c - 1) * K_PASS : c * K_PASS, cols]
+                    raw = rawp.tile([P, 4, width], BF16, tag="raw")
+                    nc.sync.dma_start(out=raw[:], in_=src.rearrange("(p t) w -> p t w", t=4))
+                    g = grp.tile([P, width, 4], BF16, align_bytes=64, tag="g")
+                    dst = g[:].rearrange("p (a i) t -> p a t i", i=4)
+                    view = raw[:].rearrange("p t (a i) -> p a t i", i=4)
+                    if u % 2 == 0:
+                        nc.vector.tensor_copy(out=dst, in_=view)
+                    else:
+                        nc.scalar.copy(out=dst, in_=view)
+                    grouped.append(g)
+                    if u > 0:
+                        quantise(codes, planes, grouped[u - 1], u - 1)
+                    if rnd == 0 and u == 3:
+                        load_x()
+            quantise(codes, planes, grouped[UNITS - 1], UNITS - 1)
+            if rnd == 0:
+                for c in range(PASSES):
+                    prep_x(c)
+
+            o_round = outp.tile([P, 2, width], F32, tag="o_round")
+            for jl in range(width // P):
+                j = d0 // P + jl
+                cols = slice(jl * P, (jl + 1) * P)
+                bank_x = ps_a.tile([P, 2 * CELLS], F32, tag="bank_x")
+                bank_y = ps_a.tile([P, 2 * CELLS], F32, tag="bank_y")
+                mx_group(bank_x[:, 0:CELLS], codes, planes, cols, 0, (0, 1, 2, 3, 4))
+                mx_group(bank_x[:, CELLS:], codes, planes, cols, 2, (1, 2, 3, 4))
+                mx_group(bank_y[:, 0:CELLS], codes, planes, cols, 1, (0, 1, 2, 3, 4))
+                mx_group(bank_y[:, CELLS:], codes, planes, cols, 2, (0,))
+
+                u_r = epi.tile([P, CELLS], F32, tag="u_r")
+                nc.vector.scalar_tensor_tensor(
+                    out=u_r[:], in0=tens[:], scalar=vec[:, j : j + 1], in1=bank_x[:, 0:CELLS], op0=ALU.mult, op1=ALU.add
+                )
+                y_sb = epi.tile([P, 2 * CELLS], F32, tag="y_sb")
+                nc.scalar.copy(out=y_sb[:], in_=bank_y[:])
+                r = epi.tile([P, CELLS], F32, tag="r")
+                nc.scalar.activation(out=r[:], in_=u_r[:], func=ACT.Sigmoid, bias=bias_r[:, j : j + 1], scale=1.0)
+                v = epi.tile([P, CELLS], F32, tag="v")
+                nc.vector.scalar_tensor_tensor(
+                    out=v[:], in0=bank_x[:, CELLS:], scalar=vec[:, 48 + j : 49 + j], in1=r[:], op0=ALU.add, op1=ALU.mult
+                )
+
+                z_ps = ps_b.tile([P, CELLS], F32, tag="z_ps")
+                flip_group(z_ps, slice(j * P, (j + 1) * P), [y_sb[:, 0:CELLS]])
+                s_ps = ps_b.tile([P, CELLS], F32, tag="s_ps")
+                flip_group(s_ps, slice(DHID + j * P, DHID + (j + 1) * P), [y_sb[:, CELLS:], v])
+
+                z = epi.tile([P, 2, P], F32, tag="z")
+                nc.scalar.activation(out=z[:].rearrange("p m d -> p (m d)"), in_=z_ps[:], func=ACT.Sigmoid)
+                cand = epi.tile([P, 2, P], F32, tag="cand")
+                nc.scalar.activation(out=cand[:].rearrange("p m d -> p (m d)"), in_=s_ps[:], func=ACT.Tanh)
+                diff = epi.tile([P, 2, P], F32, tag="diff")
+                nc.vector.tensor_sub(out=diff[:], in0=h_nat[:, :, j * P : (j + 1) * P], in1=cand[:])
+                gated = epi.tile([P, 2, P], F32, tag="gated")
+                nc.vector.tensor_mul(out=gated[:], in0=z[:], in1=diff[:])
+
+                o_ps = ps_b.tile([P, CELLS], F32, tag="o_ps")
+                nc.tensor.matmul(
+                    out=o_ps[:], lhsT=mix[:], rhs=cand[:].rearrange("p m d -> p (m d)"), start=True, stop=False
+                )
+                nc.tensor.matmul(
+                    out=o_ps[:], lhsT=mix[:], rhs=gated[:].rearrange("p m d -> p (m d)"), start=False, stop=True
+                )
+                nc.scalar.copy(out=o_round[:, :, cols], in_=o_ps[:].rearrange("p (m d) -> p m d", m=2))
+            nc.scalar.dma_start(
+                out=out[:, d0 : d0 + width].rearrange("(m p) d -> p m d", p=P), in_=o_round[:]
+            )

@@ -18,27 +18,35 @@ DOUT = 512
 DHID = 2048
 K_PASS = 512
 PASSES = 5
-GATES = 3
-UNITS = PASSES * GATES
 SYNC = 0.15
 FACTION = 32
+SUB = 512
+STORE = 512
 
-FLOPS = 2 * CELLS * (DOUT + DHID) * GATES * DHID
+FLOPS = 2 * CELLS * (DOUT + DHID) * 3 * DHID
 
-ROUNDS = ((0, 512), (512, 512), (1024, 512), (1536, 512))
+GATE_R, GATE_Z, GATE_N = 0, 1, 2
+PHASES = ((0, 0, 1024), (2, 0, 1024), (1, 0, 1024), (0, 1024, 1024), (2, 1024, 1024), (1, 1024, 512), (1, 1536, 512))
+MANUAL = True
+QLAG = 2
+VEC_TURN = (True, False)
 
 
 def tile_fractalengine_pb_kernel(tc, eng_out, tension, hiddens, w_ih, b_ih, w_hh, b_hh, out):
     nc = tc.nc
     with ExitStack() as ctx:
+        if MANUAL:
+            ctx.enter_context(tc.manual_schedule())
         const = ctx.enter_context(tc.tile_pool(name="const", bufs=1))
-        rawp = ctx.enter_context(tc.tile_pool(name="rawp", bufs=8))
-        grp = ctx.enter_context(tc.tile_pool(name="grp", bufs=4))
-        cod = ctx.enter_context(tc.tile_pool(name="cod", bufs=2))
+        rawp = ctx.enter_context(tc.tile_pool(name="rawp", bufs=4))
+        grp = ctx.enter_context(tc.tile_pool(name="grp", bufs=5))
+        gxp = ctx.enter_context(tc.tile_pool(name="gxp", bufs=2))
+        cod = ctx.enter_context(tc.tile_pool(name="cod", bufs=3))
+        keep = ctx.enter_context(tc.tile_pool(name="keep", bufs=8))
         epi = ctx.enter_context(tc.tile_pool(name="epi", bufs=3))
         outp = ctx.enter_context(tc.tile_pool(name="outp", bufs=2))
-        ps_a = ctx.enter_context(tc.psum_pool(name="ps_a", bufs=2))
-        ps_b = ctx.enter_context(tc.psum_pool(name="ps_b", bufs=1))
+        ps_mx = ctx.enter_context(tc.psum_pool(name="ps_mx", bufs=4))
+        ps_fl = ctx.enter_context(tc.psum_pool(name="ps_fl", bufs=2))
 
         ident = const.tile([P, P], F32)
         make_identity(nc, ident[:])
@@ -66,13 +74,6 @@ def tile_fractalengine_pb_kernel(tc, eng_out, tension, hiddens, w_ih, b_ih, w_hh
         nc.scalar.dma_start(out=rows[32:33, :], in_=b_ih[DHID : 3 * DHID].rearrange("(o n) -> o n", o=1))
         nc.scalar.dma_start(out=rows[64:65, 0:DHID], in_=b_hh[DHID : 2 * DHID].rearrange("(o n) -> o n", o=1))
 
-        vps = ps_b.tile([P, P], BF16, tag="spare")
-        nc.tensor.transpose(vps[:], vraw[:], ident_bf[:])
-        vec = const.tile([P, 64], F32)
-        nc.vector.tensor_copy(out=vec[:], in_=vps[:, 0:64])
-        bias_r = const.tile([P, 16], F32)
-        nc.vector.tensor_add(out=bias_r[:], in0=vec[:, 16:32], in1=vec[:, 32:48])
-
         blocks = const.tile([P, P], F32)
         nc.vector.memset(blocks[:], 0.0)
         for f in range(P // FACTION):
@@ -84,20 +85,30 @@ def tile_fractalengine_pb_kernel(tc, eng_out, tension, hiddens, w_ih, b_ih, w_hh
         nc.vector.scalar_tensor_tensor(
             out=mix[:], in0=blocks[:], scalar=SYNC / FACTION, in1=diag[:], op0=ALU.mult, op1=ALU.add
         )
+        vec = const.tile([P, 64], F32)
+        bias_r = const.tile([P, 16], F32)
+
+        def prep_vectors():
+            vps = ps_fl.tile([P, P], BF16, tag="flip")
+            nc.tensor.transpose(vps[:], vraw[:], ident_bf[:])
+            nc.vector.tensor_copy(out=vec[:], in_=vps[:, 0:64])
+            nc.vector.tensor_add(out=bias_r[:], in0=vec[:, 16:32], in1=vec[:, 32:48])
 
         h_nat = const.tile([P, 2, DHID], BF16)
         e_nat = const.tile([P, 2, DOUT], BF16)
         x_codes = const.tile([P, PASSES, CELLS], U32, align_bytes=64)
         x_scales = const.tile([P, PASSES, CELLS], U8, align_bytes=64)
+        live = {}
 
         def load_x():
             nc.sync.dma_start(out=e_nat[:], in_=eng_out.rearrange("(m p) k -> p m k", p=P))
             nc.sync.dma_start(out=h_nat[:], in_=hiddens.rearrange("(m p) k -> p m k", p=P))
 
-        def prep_x(c):
+        def x_transpose(c):
             words = (e_nat if c == 0 else h_nat)[:].bitcast(F32)
             base = 0 if c == 0 else (c - 1) * (K_PASS // 2)
-            xt = ps_a.tile([P, 2, CELLS], F32, tag="bank_x" if c % 2 == 0 else "bank_y")
+            xt = ps_mx.tile([P, 2, CELLS], F32, tag="mx")
+            live["xt", c] = xt
             for u in range(2):
                 for m in range(2):
                     nc.tensor.transpose(
@@ -105,123 +116,205 @@ def tile_fractalengine_pb_kernel(tc, eng_out, tension, hiddens, w_ih, b_ih, w_hh
                         words[:, m, base + u : base + K_PASS // 2 : 2],
                         ident[:],
                     )
-            gx = grp.tile([P, CELLS, 4], BF16, align_bytes=64, tag="gx")
-            nc.vector.tensor_copy(out=gx[:].bitcast(F32), in_=xt[:].rearrange("p u n -> p n u"))
+
+        def x_copy(c):
+            gx = gxp.tile([P, CELLS, 4], BF16, align_bytes=64, tag="gx")
+            live["gx", c] = gx
+            nc.scalar.copy(out=gx[:].bitcast(F32), in_=live["xt", c][:].rearrange("p u n -> p n u"))
+
+        def x_quantise(c):
             nc.vector.quantize_mx(
                 out=x_codes[:, c, :].bitcast(FP8X4),
                 scales=x_scales[:, c, :],
-                in_=gx[:].rearrange("p n t -> p (n t)"),
+                in_=live["gx", c][:].rearrange("p n t -> p (n t)"),
             )
 
-        def quantise(codes, planes, g, u):
+        def open_phase(ph, width):
+            codes = cod.tile([P, PASSES, width], U32, align_bytes=64, tag="codes")
+            planes = cod.tile([P, PASSES, width], U8, align_bytes=64, tag="planes")
+            live["codes", ph] = codes
+            live["planes", ph] = planes
+
+        def load(ph, c, gate, d0, width, pieces):
+            raw = rawp.tile([P, 4, width], BF16, tag="raw")
+            live["raw", ph, c] = raw
+            step = width // pieces
+            for i in range(pieces):
+                lo = gate * DHID + d0 + i * step
+                src = w_ih[0:K_PASS, lo : lo + step] if c == 0 else w_hh[(c - 1) * K_PASS : c * K_PASS, lo : lo + step]
+                nc.sync.dma_start(
+                    out=raw[:, :, i * step : (i + 1) * step], in_=src.rearrange("(p t) w -> p t w", t=4)
+                )
+
+        def regroup(ph, c, hh, slot):
+            g = grp.tile([P, SUB, 4], BF16, align_bytes=64, tag="g")
+            live["g", slot] = g
+            dst = g[:].rearrange("p (a i) t -> p a t i", i=4)
+            view = live["raw", ph, c][:, :, hh * SUB : (hh + 1) * SUB].rearrange("p t (a i) -> p a t i", i=4)
+            if VEC_TURN[slot % len(VEC_TURN)]:
+                nc.vector.tensor_copy(out=dst, in_=view)
+            else:
+                nc.scalar.copy(out=dst, in_=view)
+
+        def quantise(ph, c, hh, slot):
             nc.vector.quantize_mx(
-                out=codes[:, u, :].bitcast(FP8X4),
-                scales=planes[:, u, :],
-                in_=g[:].rearrange("p w t -> p (w t)"),
+                out=live["codes", ph][:, c, hh * SUB : (hh + 1) * SUB].bitcast(FP8X4),
+                scales=live["planes", ph][:, c, hh * SUB : (hh + 1) * SUB],
+                in_=live["g", slot][:].rearrange("p w t -> p (w t)"),
             )
 
-        def mx_group(acc, codes, planes, cols, gate, passes):
+        def mx_group(name, j, ph, i, passes):
+            acc = ps_mx.tile([P, CELLS], F32, tag="mx")
+            live[name, j] = acc
+            cols = slice(i * P, (i + 1) * P)
             for c in passes:
-                u = c * GATES + gate
                 nc.tensor.matmul_mx(
-                    out=acc,
-                    lhsT=codes[:, u, cols].bitcast(FP8X4),
-                    lhsT_scale=planes[:, u, cols],
+                    out=acc[:],
+                    lhsT=live["codes", ph][:, c, cols].bitcast(FP8X4),
+                    lhsT_scale=live["planes", ph][:, c, cols],
                     rhs=x_codes[:, c, :].bitcast(FP8X4),
                     rhs_scale=x_scales[:, c, :],
                     start=(c == passes[0]),
                     stop=(c == passes[-1]),
                 )
 
-        def flip_group(acc, row_cols, parts):
+        def flip_group(name, j, row0, parts):
+            acc = ps_fl.tile([P, CELLS], F32, tag="flip")
+            live[name, j] = acc
             for m in range(2):
                 half = slice(m * P, (m + 1) * P)
-                nc.tensor.matmul(out=acc[:, half], lhsT=lift[:, half], rhs=rows[:, row_cols], start=True, stop=False)
-                for i, part in enumerate(parts):
+                nc.tensor.matmul(
+                    out=acc[:, half], lhsT=lift[:, half], rhs=rows[:, row0 + j * P : row0 + (j + 1) * P],
+                    start=True, stop=False,
+                )
+                for k, part in enumerate(parts):
                     nc.tensor.matmul(
-                        out=acc[:, half],
-                        lhsT=part[:, half],
-                        rhs=ident[:],
-                        is_transpose=True,
-                        start=False,
-                        stop=(i == len(parts) - 1),
+                        out=acc[:, half], lhsT=part[:, half], rhs=ident[:], is_transpose=True,
+                        start=False, stop=(k == len(parts) - 1),
                     )
 
-        for rnd, (d0, width) in enumerate(ROUNDS):
-            codes = cod.tile([P, UNITS, width], U32, align_bytes=64, tag="codes")
-            planes = cod.tile([P, UNITS, width], U8, align_bytes=64, tag="planes")
-            grouped = []
-
-            for c in range(PASSES):
-                for gate in range(GATES):
-                    u = c * GATES + gate
-                    cols = slice(gate * DHID + d0, gate * DHID + d0 + width)
-                    src = w_ih[0:K_PASS, cols] if c == 0 else w_hh[(c - 1) * K_PASS : c * K_PASS, cols]
-                    raw = rawp.tile([P, 4, width], BF16, tag="raw")
-                    nc.sync.dma_start(out=raw[:], in_=src.rearrange("(p t) w -> p t w", t=4))
-                    g = grp.tile([P, width, 4], BF16, align_bytes=64, tag="g")
-                    dst = g[:].rearrange("p (a i) t -> p a t i", i=4)
-                    view = raw[:].rearrange("p t (a i) -> p a t i", i=4)
-                    if u % 2 == 0:
-                        nc.vector.tensor_copy(out=dst, in_=view)
-                    else:
-                        nc.scalar.copy(out=dst, in_=view)
-                    grouped.append(g)
-                    if u > 0:
-                        quantise(codes, planes, grouped[u - 1], u - 1)
-                    if rnd == 0 and u == 3:
-                        load_x()
-            quantise(codes, planes, grouped[UNITS - 1], UNITS - 1)
-            if rnd == 0:
-                for c in range(PASSES):
-                    prep_x(c)
-
-            o_round = outp.tile([P, 2, width], F32, tag="o_round")
-            for jl in range(width // P):
-                j = d0 // P + jl
-                cols = slice(jl * P, (jl + 1) * P)
-                bank_x = ps_a.tile([P, 2 * CELLS], F32, tag="bank_x")
-                bank_y = ps_a.tile([P, 2 * CELLS], F32, tag="bank_y")
-                mx_group(bank_x[:, 0:CELLS], codes, planes, cols, 0, (0, 1, 2, 3, 4))
-                mx_group(bank_x[:, CELLS:], codes, planes, cols, 2, (1, 2, 3, 4))
-                mx_group(bank_y[:, 0:CELLS], codes, planes, cols, 1, (0, 1, 2, 3, 4))
-                mx_group(bank_y[:, CELLS:], codes, planes, cols, 2, (0,))
-
-                u_r = epi.tile([P, CELLS], F32, tag="u_r")
-                nc.vector.scalar_tensor_tensor(
-                    out=u_r[:], in0=tens[:], scalar=vec[:, j : j + 1], in1=bank_x[:, 0:CELLS], op0=ALU.mult, op1=ALU.add
-                )
-                y_sb = epi.tile([P, 2 * CELLS], F32, tag="y_sb")
-                nc.scalar.copy(out=y_sb[:], in_=bank_y[:])
-                r = epi.tile([P, CELLS], F32, tag="r")
-                nc.scalar.activation(out=r[:], in_=u_r[:], func=ACT.Sigmoid, bias=bias_r[:, j : j + 1], scale=1.0)
-                v = epi.tile([P, CELLS], F32, tag="v")
-                nc.vector.scalar_tensor_tensor(
-                    out=v[:], in0=bank_x[:, CELLS:], scalar=vec[:, 48 + j : 49 + j], in1=r[:], op0=ALU.add, op1=ALU.mult
-                )
-
-                z_ps = ps_b.tile([P, CELLS], F32, tag="z_ps")
-                flip_group(z_ps, slice(j * P, (j + 1) * P), [y_sb[:, 0:CELLS]])
-                s_ps = ps_b.tile([P, CELLS], F32, tag="s_ps")
-                flip_group(s_ps, slice(DHID + j * P, DHID + (j + 1) * P), [y_sb[:, CELLS:], v])
-
-                z = epi.tile([P, 2, P], F32, tag="z")
-                nc.scalar.activation(out=z[:].rearrange("p m d -> p (m d)"), in_=z_ps[:], func=ACT.Sigmoid)
-                cand = epi.tile([P, 2, P], F32, tag="cand")
-                nc.scalar.activation(out=cand[:].rearrange("p m d -> p (m d)"), in_=s_ps[:], func=ACT.Tanh)
-                diff = epi.tile([P, 2, P], F32, tag="diff")
-                nc.vector.tensor_sub(out=diff[:], in0=h_nat[:, :, j * P : (j + 1) * P], in1=cand[:])
-                gated = epi.tile([P, 2, P], F32, tag="gated")
-                nc.vector.tensor_mul(out=gated[:], in0=z[:], in1=diff[:])
-
-                o_ps = ps_b.tile([P, CELLS], F32, tag="o_ps")
-                nc.tensor.matmul(
-                    out=o_ps[:], lhsT=mix[:], rhs=cand[:].rearrange("p m d -> p (m d)"), start=True, stop=False
-                )
-                nc.tensor.matmul(
-                    out=o_ps[:], lhsT=mix[:], rhs=gated[:].rearrange("p m d -> p (m d)"), start=False, stop=True
-                )
-                nc.scalar.copy(out=o_round[:, :, cols], in_=o_ps[:].rearrange("p (m d) -> p m d", m=2))
-            nc.scalar.dma_start(
-                out=out[:, d0 : d0 + width].rearrange("(m p) d -> p m d", p=P), in_=o_round[:]
+        def r_add(j):
+            u_r = epi.tile([P, CELLS], F32, tag="u_r")
+            live["u_r", j] = u_r
+            nc.vector.scalar_tensor_tensor(
+                out=u_r[:], in0=tens[:], scalar=vec[:, j : j + 1], in1=live["ps_r", j][:], op0=ALU.mult, op1=ALU.add
             )
+
+        def r_gate(j):
+            r = keep.tile([P, CELLS], F32, tag="r")
+            live["r", j] = r
+            nc.scalar.activation(out=r[:], in_=live["u_r", j][:], func=ACT.Sigmoid, bias=bias_r[:, j : j + 1], scale=1.0)
+
+        def n_out(j):
+            a_i = epi.tile([P, CELLS], F32, tag="a_i")
+            live["a_i", j] = a_i
+            nc.scalar.copy(out=a_i[:], in_=live["ps_i", j][:])
+            v = epi.tile([P, CELLS], F32, tag="v")
+            live["v", j] = v
+            nc.vector.scalar_tensor_tensor(
+                out=v[:], in0=live["ps_h", j][:], scalar=vec[:, 48 + j : 49 + j], in1=live["r", j][:],
+                op0=ALU.add, op1=ALU.mult,
+            )
+
+        def n_tanh(j):
+            cand = keep.tile([P, 2, P], F32, tag="cand")
+            live["cand", j] = cand
+            nc.scalar.activation(out=cand[:].rearrange("p m d -> p (m d)"), in_=live["ps_s", j][:], func=ACT.Tanh)
+
+        def n_diff(j):
+            diff = keep.tile([P, 2, P], F32, tag="diff")
+            live["diff", j] = diff
+            nc.vector.tensor_sub(out=diff[:], in0=h_nat[:, :, j * P : (j + 1) * P], in1=live["cand", j][:])
+
+        def z_out(j):
+            a_z = epi.tile([P, CELLS], F32, tag="a_z")
+            live["a_z", j] = a_z
+            nc.scalar.copy(out=a_z[:], in_=live["ps_z", j][:])
+
+        def z_gate(j):
+            z = epi.tile([P, 2, P], F32, tag="z")
+            live["z", j] = z
+            nc.scalar.activation(out=z[:].rearrange("p m d -> p (m d)"), in_=live["ps_zn", j][:], func=ACT.Sigmoid)
+
+        def z_mul(j):
+            gated = epi.tile([P, 2, P], F32, tag="gated")
+            live["gated", j] = gated
+            nc.vector.tensor_mul(out=gated[:], in0=live["z", j][:], in1=live["diff", j][:])
+
+        def mix_up(j):
+            o_ps = ps_fl.tile([P, CELLS], F32, tag="o_ps")
+            live["o_ps", j] = o_ps
+            nc.tensor.matmul(
+                out=o_ps[:], lhsT=mix[:], rhs=live["cand", j][:].rearrange("p m d -> p (m d)"), start=True, stop=False
+            )
+            nc.tensor.matmul(
+                out=o_ps[:], lhsT=mix[:], rhs=live["gated", j][:].rearrange("p m d -> p (m d)"), start=False, stop=True
+            )
+
+        def finish(j):
+            per = STORE // P
+            if j % per == 0:
+                o_sb = outp.tile([P, 2, STORE], F32, tag="o_sb")
+                live["o_sb", j // per] = o_sb
+            o_sb = live["o_sb", j // per]
+            nc.scalar.copy(
+                out=o_sb[:, :, (j % per) * P : (j % per + 1) * P],
+                in_=live["o_ps", j][:].rearrange("p (m d) -> p m d", m=2),
+            )
+            if j % per == per - 1:
+                lo = (j // per) * STORE
+                nc.scalar.dma_start(out=out[:, lo : lo + STORE].rearrange("(m p) d -> p m d", p=P), in_=o_sb[:])
+
+        chain = {}
+        bulk = {}
+
+        def at(table, slot, fn):
+            if slot not in table:
+                table[slot] = []
+            table[slot].append(fn)
+
+        at(bulk, 3, load_x)
+        at(chain, 4, prep_vectors)
+        for c in range(PASSES):
+            at(chain, 5 + c, lambda c=c: x_transpose(c))
+            at(chain, 6 + c, lambda c=c: x_copy(c))
+            at(chain, 7 + c, lambda c=c: x_quantise(c))
+
+        slot = 0
+        for ph, (gate, d0, width) in enumerate(PHASES):
+            at(bulk, slot, lambda ph=ph, width=width: open_phase(ph, width))
+            for c in range(PASSES):
+                pieces = 2 if slot == 0 else 1
+                at(bulk, slot, lambda ph=ph, c=c, gate=gate, d0=d0, width=width, pieces=pieces: load(ph, c, gate, d0, width, pieces))
+                for hh in range(width // SUB):
+                    at(bulk, slot, lambda ph=ph, c=c, hh=hh, slot=slot: regroup(ph, c, hh, slot))
+                    at(bulk, slot + QLAG, lambda ph=ph, c=c, hh=hh, slot=slot: quantise(ph, c, hh, slot))
+                    slot += 1
+            for i in range(width // P):
+                j = d0 // P + i
+                t0 = slot + QLAG + i
+                if gate == GATE_R:
+                    at(chain, t0, lambda j=j, ph=ph, i=i: mx_group("ps_r", j, ph, i, (0, 1, 2, 3, 4)))
+                    at(chain, t0 + 1, lambda j=j: r_add(j))
+                    at(chain, t0 + 2, lambda j=j: r_gate(j))
+                elif gate == GATE_N:
+                    at(chain, t0, lambda j=j, ph=ph, i=i: mx_group("ps_i", j, ph, i, (0,)))
+                    at(chain, t0, lambda j=j, ph=ph, i=i: mx_group("ps_h", j, ph, i, (1, 2, 3, 4)))
+                    at(chain, t0 + 1, lambda j=j: n_out(j))
+                    at(chain, t0 + 2, lambda j=j: flip_group("ps_s", j, DHID, [live["a_i", j], live["v", j]]))
+                    at(chain, t0 + 3, lambda j=j: n_tanh(j))
+                    at(chain, t0 + 4, lambda j=j: n_diff(j))
+                else:
+                    at(chain, t0, lambda j=j, ph=ph, i=i: mx_group("ps_z", j, ph, i, (0, 1, 2, 3, 4)))
+                    at(chain, t0 + 1, lambda j=j: z_out(j))
+                    at(chain, t0 + 2, lambda j=j: flip_group("ps_zn", j, 0, [live["a_z", j]]))
+                    at(chain, t0 + 3, lambda j=j: z_gate(j))
+                    at(chain, t0 + 4, lambda j=j: z_mul(j))
+                    at(chain, t0 + 5, lambda j=j: mix_up(j))
+                    at(chain, t0 + 6, lambda j=j: finish(j))
+
+        for s in range(slot + 32):
+            for fn in chain.get(s, []):
+                fn()
+            for fn in bulk.get(s, []):
+                fn()

@@ -13,308 +13,330 @@ ALU = mybir.AluOpType
 ACT = mybir.ActivationFunctionType
 
 P = 128
+PACK = 4
+K_PASS = P * PACK
 CELLS = 256
+HALVES = CELLS // P
 DOUT = 512
 DHID = 2048
-K_PASS = 512
-PASSES = 5
+PASSES = (DOUT + DHID) // K_PASS
+ALL_PASSES = tuple(range(PASSES))
 SYNC = 0.15
 FACTION = 32
-SUB = 512
-STORE = 512
+GATE_R, GATE_Z, GATE_N = 0, 1, 2
 
 FLOPS = 2 * CELLS * (DOUT + DHID) * 3 * DHID
 
-GATE_R, GATE_Z, GATE_N = 0, 1, 2
-PHASES = ((0, 0, 1024), (2, 0, 1024), (1, 0, 1024), (0, 1024, 1024), (2, 1024, 1024), (1, 1024, 512), (1, 1536, 512))
-MANUAL = True
-QLAG = 2
-VEC_TURN = (True, False)
+GROUPS = ((0, 1024), (1024, 512), (1536, 512))
+LAST_Z_SPLIT = 2
+SUB = 512
+
+QUANTISE_LAG = 2
+X_LOAD_SLOT = 3
+X_SLOT = 5
+VECTORS_SLOT = 10
+DRAIN_SLOTS = 16
 
 
 def tile_fractalengine_pb_kernel(tc, eng_out, tension, hiddens, w_ih, b_ih, w_hh, b_hh, out):
     nc = tc.nc
     with ExitStack() as ctx:
-        if MANUAL:
-            ctx.enter_context(tc.manual_schedule())
+        ctx.enter_context(tc.manual_schedule())
         const = ctx.enter_context(tc.tile_pool(name="const", bufs=1))
-        rawp = ctx.enter_context(tc.tile_pool(name="rawp", bufs=4))
-        grp = ctx.enter_context(tc.tile_pool(name="grp", bufs=5))
-        gxp = ctx.enter_context(tc.tile_pool(name="gxp", bufs=2))
-        cod = ctx.enter_context(tc.tile_pool(name="cod", bufs=3))
-        keep = ctx.enter_context(tc.tile_pool(name="keep", bufs=8))
-        epi = ctx.enter_context(tc.tile_pool(name="epi", bufs=3))
-        outp = ctx.enter_context(tc.tile_pool(name="outp", bufs=2))
-        ps_mx = ctx.enter_context(tc.psum_pool(name="ps_mx", bufs=4))
-        ps_fl = ctx.enter_context(tc.psum_pool(name="ps_fl", bufs=2))
+        raw_pool = ctx.enter_context(tc.tile_pool(name="raw_pool", bufs=PASSES))
+        grouped_pool = ctx.enter_context(tc.tile_pool(name="grouped_pool", bufs=QUANTISE_LAG + 3))
+        x_pool = ctx.enter_context(tc.tile_pool(name="x_pool", bufs=2))
+        code_pool = ctx.enter_context(tc.tile_pool(name="code_pool", bufs=3))
+        keep_pool = ctx.enter_context(tc.tile_pool(name="keep_pool", bufs=max(group[1] for group in GROUPS) // P))
+        step_pool = ctx.enter_context(tc.tile_pool(name="step_pool", bufs=3))
+        out_pool = ctx.enter_context(tc.tile_pool(name="out_pool", bufs=2))
+        mx_psum = ctx.enter_context(tc.psum_pool(name="mx_psum", bufs=4))
+        plain_psum = ctx.enter_context(tc.psum_pool(name="plain_psum", bufs=2))
 
         ident = const.tile([P, P], F32)
         make_identity(nc, ident[:])
         ident_bf = const.tile([P, P], BF16)
         make_identity(nc, ident_bf[:])
 
-        vraw = const.tile([P, P], BF16)
-        nc.vector.memset(vraw[:].bitcast(I32), 0)
+        blocks_all = DHID // P
+        vec_rows = const.tile([P, P], BF16)
+        nc.vector.memset(vec_rows[:].bitcast(I32), 0)
         lift = const.tile([P, CELLS], BF16)
         nc.vector.memset(lift[:].bitcast(I32), 0)
         nc.vector.memset(lift[32:64, :], 1.0)
         nc.vector.memset(lift[64:96, :], 1.0)
         rows = const.tile([P, 2 * DHID], BF16)
         nc.vector.memset(rows[:].bitcast(I32), 0)
-        tens = const.tile([P, CELLS], BF16)
+        tension_all = const.tile([P, CELLS], BF16)
 
-        last = w_ih[DOUT : DOUT + 1, :]
-        nc.scalar.dma_start(out=vraw[0:16, :], in_=last[:, 0:DHID].rearrange("o (r c) -> (o r) c", c=P))
-        nc.scalar.dma_start(out=vraw[16:32, :], in_=b_ih[0:DHID].rearrange("(r c) -> r c", c=P))
-        nc.scalar.dma_start(out=vraw[32:48, :], in_=b_hh[0:DHID].rearrange("(r c) -> r c", c=P))
-        nc.scalar.dma_start(out=vraw[48:64, :], in_=b_hh[2 * DHID : 3 * DHID].rearrange("(r c) -> r c", c=P))
-        nc.scalar.dma_start(out=tens[:], in_=tension.partition_broadcast(P))
-        nc.scalar.dma_start(out=lift[0:1, :], in_=tension.rearrange("(o n) -> o n", o=1))
-        nc.scalar.dma_start(out=rows[0:1, :], in_=last[:, DHID : 3 * DHID])
-        nc.scalar.dma_start(out=rows[32:33, :], in_=b_ih[DHID : 3 * DHID].rearrange("(o n) -> o n", o=1))
-        nc.scalar.dma_start(out=rows[64:65, 0:DHID], in_=b_hh[DHID : 2 * DHID].rearrange("(o n) -> o n", o=1))
+        last_row = w_ih[DOUT : DOUT + 1, :]
+        nc.gpsimd.dma_start(out=vec_rows[0:16, :], in_=last_row[:, 0:DHID].rearrange("o (r c) -> (o r) c", c=P))
+        nc.gpsimd.dma_start(out=vec_rows[16:32, :], in_=b_ih[0:DHID].rearrange("(r c) -> r c", c=P))
+        nc.gpsimd.dma_start(out=vec_rows[32:48, :], in_=b_hh[0:DHID].rearrange("(r c) -> r c", c=P))
+        nc.gpsimd.dma_start(out=vec_rows[48:64, :], in_=b_hh[2 * DHID : 3 * DHID].rearrange("(r c) -> r c", c=P))
+        nc.gpsimd.dma_start(out=tension_all[:], in_=tension.partition_broadcast(P))
+        nc.gpsimd.dma_start(out=lift[0:1, :], in_=tension.rearrange("(o n) -> o n", o=1))
+        nc.gpsimd.dma_start(out=rows[0:1, :], in_=last_row[:, DHID : 3 * DHID])
+        nc.gpsimd.dma_start(out=rows[32:33, :], in_=b_ih[DHID : 3 * DHID].rearrange("(o n) -> o n", o=1))
+        nc.gpsimd.dma_start(out=rows[64:65, 0:DHID], in_=b_hh[DHID : 2 * DHID].rearrange("(o n) -> o n", o=1))
 
-        blocks = const.tile([P, P], F32)
-        nc.vector.memset(blocks[:], 0.0)
+        same_faction = const.tile([P, P], F32)
+        nc.vector.memset(same_faction[:], 0.0)
         for f in range(P // FACTION):
-            span = slice(f * FACTION, (f + 1) * FACTION)
-            nc.vector.memset(blocks[span, span], 1.0)
-        diag = const.tile([P, P], F32)
-        nc.vector.tensor_scalar_mul(out=diag[:], in0=ident[:], scalar1=1.0 - SYNC)
+            members = slice(f * FACTION, (f + 1) * FACTION)
+            nc.vector.memset(same_faction[members, members], 1.0)
+        own = const.tile([P, P], F32)
+        nc.vector.tensor_scalar_mul(out=own[:], in0=ident[:], scalar1=1.0 - SYNC)
         mix = const.tile([P, P], F32)
         nc.vector.scalar_tensor_tensor(
-            out=mix[:], in0=blocks[:], scalar=SYNC / FACTION, in1=diag[:], op0=ALU.mult, op1=ALU.add
+            out=mix[:], in0=same_faction[:], scalar=SYNC / FACTION, in1=own[:], op0=ALU.mult, op1=ALU.add
         )
-        vec = const.tile([P, 64], F32)
-        bias_r = const.tile([P, 16], F32)
 
-        def prep_vectors():
-            vps = ps_fl.tile([P, P], BF16, tag="flip")
-            nc.tensor.transpose(vps[:], vraw[:], ident_bf[:])
-            nc.vector.tensor_copy(out=vec[:], in_=vps[:, 0:64])
-            nc.vector.tensor_add(out=bias_r[:], in0=vec[:, 16:32], in1=vec[:, 32:48])
+        vec = const.tile([P, 4 * blocks_all], F32)
+        bias_r = const.tile([P, blocks_all], F32)
 
-        h_nat = const.tile([P, 2, DHID], BF16)
-        e_nat = const.tile([P, 2, DOUT], BF16)
-        x_codes = const.tile([P, PASSES, CELLS], U32, align_bytes=64)
-        x_scales = const.tile([P, PASSES, CELLS], U8, align_bytes=64)
+        def turn_vectors():
+            turned = plain_psum.tile([P, P], BF16, tag="turned")
+            nc.tensor.transpose(turned[:], vec_rows[:], ident_bf[:])
+            nc.vector.tensor_copy(out=vec[:], in_=turned[:, 0 : 4 * blocks_all])
+            nc.vector.tensor_add(
+                out=bias_r[:], in0=vec[:, blocks_all : 2 * blocks_all], in1=vec[:, 2 * blocks_all : 3 * blocks_all]
+            )
+
         live = {}
 
+        h_cells = const.tile([P, HALVES, DHID], BF16)
+        e_cells = const.tile([P, HALVES, DOUT], BF16)
+        x_codes = const.tile([P, PASSES, CELLS], U32, align_bytes=64)
+        x_scales = const.tile([P, PASSES, CELLS], U8, align_bytes=64)
+
         def load_x():
-            nc.sync.dma_start(out=e_nat[:], in_=eng_out.rearrange("(m p) k -> p m k", p=P))
-            nc.sync.dma_start(out=h_nat[:], in_=hiddens.rearrange("(m p) k -> p m k", p=P))
+            nc.sync.dma_start(out=e_cells[:], in_=eng_out.rearrange("(m p) k -> p m k", p=P))
+            nc.sync.dma_start(out=h_cells[:], in_=hiddens.rearrange("(m p) k -> p m k", p=P))
 
         def x_transpose(c):
-            words = (e_nat if c == 0 else h_nat)[:].bitcast(F32)
+            words = (e_cells if c == 0 else h_cells)[:].bitcast(F32)
             base = 0 if c == 0 else (c - 1) * (K_PASS // 2)
-            xt = ps_mx.tile([P, 2, CELLS], F32, tag="mx")
-            live["xt", c] = xt
+            planes = mx_psum.tile([P, 2, CELLS], F32, tag="mx")
+            live["x_planes", c] = planes
             for u in range(2):
-                for m in range(2):
+                for m in range(HALVES):
                     nc.tensor.transpose(
-                        xt[:, u, m * P : (m + 1) * P],
-                        words[:, m, base + u : base + K_PASS // 2 : 2],
-                        ident[:],
+                        planes[:, u, m * P : (m + 1) * P], words[:, m, base + u : base + K_PASS // 2 : 2], ident[:]
                     )
 
         def x_copy(c):
-            gx = gxp.tile([P, CELLS, 4], BF16, align_bytes=64, tag="gx")
-            live["gx", c] = gx
-            nc.scalar.copy(out=gx[:].bitcast(F32), in_=live["xt", c][:].rearrange("p u n -> p n u"))
+            x_grouped = x_pool.tile([P, CELLS, PACK], BF16, align_bytes=64, tag="x_grouped")
+            live["x_grouped", c] = x_grouped
+            nc.scalar.copy(out=x_grouped[:].bitcast(F32), in_=live["x_planes", c][:].rearrange("p u n -> p n u"))
 
         def x_quantise(c):
             nc.vector.quantize_mx(
                 out=x_codes[:, c, :].bitcast(FP8X4),
                 scales=x_scales[:, c, :],
-                in_=live["gx", c][:].rearrange("p n t -> p (n t)"),
+                in_=live["x_grouped", c][:].rearrange("p n t -> p (n t)"),
             )
+
+        def load_weights(gate, g0, span, c):
+            raw = raw_pool.tile([P, PACK, span], BF16, tag="raw")
+            live["raw", gate, g0, c] = raw
+            cols = slice(gate * DHID + g0, gate * DHID + g0 + span)
+            src = w_ih[0:K_PASS, cols] if c == 0 else w_hh[(c - 1) * K_PASS : c * K_PASS, cols]
+            nc.sync.dma_start(out=raw[:], in_=src.rearrange("(p t) w -> p t w", t=PACK))
 
         def open_phase(ph, width):
-            codes = cod.tile([P, PASSES, width], U32, align_bytes=64, tag="codes")
-            planes = cod.tile([P, PASSES, width], U8, align_bytes=64, tag="planes")
+            codes = code_pool.tile([P, PASSES, width], U32, align_bytes=64, tag="codes")
+            scales = code_pool.tile([P, PASSES, width], U8, align_bytes=64, tag="scales")
             live["codes", ph] = codes
-            live["planes", ph] = planes
+            live["scales", ph] = scales
 
-        def load(ph, c, gate, d0, width, pieces):
-            raw = rawp.tile([P, 4, width], BF16, tag="raw")
-            live["raw", ph, c] = raw
-            step = width // pieces
-            for i in range(pieces):
-                lo = gate * DHID + d0 + i * step
-                src = w_ih[0:K_PASS, lo : lo + step] if c == 0 else w_hh[(c - 1) * K_PASS : c * K_PASS, lo : lo + step]
-                nc.sync.dma_start(
-                    out=raw[:, :, i * step : (i + 1) * step], in_=src.rearrange("(p t) w -> p t w", t=4)
-                )
-
-        def regroup(ph, c, hh, slot):
-            g = grp.tile([P, SUB, 4], BF16, align_bytes=64, tag="g")
-            live["g", slot] = g
-            dst = g[:].rearrange("p (a i) t -> p a t i", i=4)
-            view = live["raw", ph, c][:, :, hh * SUB : (hh + 1) * SUB].rearrange("p t (a i) -> p a t i", i=4)
-            if VEC_TURN[slot % len(VEC_TURN)]:
-                nc.vector.tensor_copy(out=dst, in_=view)
+        def regroup(slot, raw, lo, sub):
+            grouped = grouped_pool.tile([P, sub, PACK], BF16, align_bytes=64, tag="grouped")
+            live["grouped", slot] = grouped
+            dst = grouped[:].rearrange("p (a i) t -> p a t i", i=4)
+            src = raw[:, :, lo : lo + sub].rearrange("p t (a i) -> p a t i", i=4)
+            if slot % 2 == 0:
+                nc.vector.tensor_copy(out=dst, in_=src)
             else:
-                nc.scalar.copy(out=dst, in_=view)
+                nc.scalar.copy(out=dst, in_=src)
 
-        def quantise(ph, c, hh, slot):
+        def quantise(slot, ph, c, lo, sub):
             nc.vector.quantize_mx(
-                out=live["codes", ph][:, c, hh * SUB : (hh + 1) * SUB].bitcast(FP8X4),
-                scales=live["planes", ph][:, c, hh * SUB : (hh + 1) * SUB],
-                in_=live["g", slot][:].rearrange("p w t -> p (w t)"),
+                out=live["codes", ph][:, c, lo : lo + sub].bitcast(FP8X4),
+                scales=live["scales", ph][:, c, lo : lo + sub],
+                in_=live["grouped", slot][:].rearrange("p w t -> p (w t)"),
             )
 
-        def mx_group(name, j, ph, i, passes):
-            acc = ps_mx.tile([P, CELLS], F32, tag="mx")
-            live[name, j] = acc
-            cols = slice(i * P, (i + 1) * P)
+        def mx_passes(name, ph, i, j, group, passes):
+            if passes[0] == group[0]:
+                acc = mx_psum.tile([P, CELLS], F32, tag="mx")
+                live[name, j] = acc
             for c in passes:
                 nc.tensor.matmul_mx(
-                    out=acc[:],
-                    lhsT=live["codes", ph][:, c, cols].bitcast(FP8X4),
-                    lhsT_scale=live["planes", ph][:, c, cols],
+                    out=live[name, j][:],
+                    lhsT=live["codes", ph][:, c, i * P : (i + 1) * P].bitcast(FP8X4),
+                    lhsT_scale=live["scales", ph][:, c, i * P : (i + 1) * P],
                     rhs=x_codes[:, c, :].bitcast(FP8X4),
                     rhs_scale=x_scales[:, c, :],
-                    start=(c == passes[0]),
-                    stop=(c == passes[-1]),
+                    start=(c == group[0]),
+                    stop=(c == group[-1]),
                 )
 
-        def flip_group(name, j, row0, parts):
-            acc = ps_fl.tile([P, CELLS], F32, tag="flip")
+        def turn(name, j, row0, parts):
+            acc = plain_psum.tile([P, CELLS], F32, tag="turned")
             live[name, j] = acc
-            for m in range(2):
+            for m in range(HALVES):
                 half = slice(m * P, (m + 1) * P)
                 nc.tensor.matmul(
                     out=acc[:, half], lhsT=lift[:, half], rhs=rows[:, row0 + j * P : row0 + (j + 1) * P],
                     start=True, stop=False,
                 )
-                for k, part in enumerate(parts):
+                for part in parts:
                     nc.tensor.matmul(
                         out=acc[:, half], lhsT=part[:, half], rhs=ident[:], is_transpose=True,
-                        start=False, stop=(k == len(parts) - 1),
+                        start=False, stop=(part is parts[-1]),
                     )
 
-        def r_add(j):
-            u_r = epi.tile([P, CELLS], F32, tag="u_r")
-            live["u_r", j] = u_r
+        def r_matmuls(ph, i, j):
+            mx_passes("ps_r", ph, i, j, ALL_PASSES, ALL_PASSES)
+
+        def r_add(ph, i, j):
+            r_in = step_pool.tile([P, CELLS], F32, tag="r_in")
+            live["r_in", j] = r_in
             nc.vector.scalar_tensor_tensor(
-                out=u_r[:], in0=tens[:], scalar=vec[:, j : j + 1], in1=live["ps_r", j][:], op0=ALU.mult, op1=ALU.add
+                out=r_in[:], in0=tension_all[:], scalar=vec[:, j : j + 1], in1=live["ps_r", j][:],
+                op0=ALU.mult, op1=ALU.add,
             )
 
-        def r_gate(j):
-            r = keep.tile([P, CELLS], F32, tag="r")
+        def r_gate(ph, i, j):
+            r = keep_pool.tile([P, CELLS], F32, tag="r")
             live["r", j] = r
-            nc.scalar.activation(out=r[:], in_=live["u_r", j][:], func=ACT.Sigmoid, bias=bias_r[:, j : j + 1], scale=1.0)
+            nc.scalar.activation(out=r[:], in_=live["r_in", j][:], func=ACT.Sigmoid, bias=bias_r[:, j : j + 1], scale=1.0)
 
-        def n_out(j):
-            a_i = epi.tile([P, CELLS], F32, tag="a_i")
-            live["a_i", j] = a_i
-            nc.scalar.copy(out=a_i[:], in_=live["ps_i", j][:])
-            v = epi.tile([P, CELLS], F32, tag="v")
-            live["v", j] = v
+        def n_matmuls(ph, i, j):
+            mx_passes("ps_inn", ph, i, j, ALL_PASSES[:1], ALL_PASSES[:1])
+            mx_passes("ps_hn", ph, i, j, ALL_PASSES[1:], ALL_PASSES[1:])
+
+        def n_out(ph, i, j):
+            inn = step_pool.tile([P, CELLS], F32, tag="inn")
+            live["inn", j] = inn
+            nc.scalar.copy(out=inn[:], in_=live["ps_inn", j][:])
+            r_hn = step_pool.tile([P, CELLS], F32, tag="r_hn")
+            live["r_hn", j] = r_hn
             nc.vector.scalar_tensor_tensor(
-                out=v[:], in0=live["ps_h", j][:], scalar=vec[:, 48 + j : 49 + j], in1=live["r", j][:],
-                op0=ALU.add, op1=ALU.mult,
+                out=r_hn[:], in0=live["ps_hn", j][:], scalar=vec[:, 3 * blocks_all + j : 3 * blocks_all + j + 1],
+                in1=live["r", j][:], op0=ALU.add, op1=ALU.mult,
             )
 
-        def n_tanh(j):
-            cand = keep.tile([P, 2, P], F32, tag="cand")
+        def n_turn(ph, i, j):
+            turn("ps_cand", j, DHID, [live["inn", j], live["r_hn", j]])
+
+        def n_tanh(ph, i, j):
+            cand = keep_pool.tile([P, HALVES, P], F32, tag="cand")
             live["cand", j] = cand
-            nc.scalar.activation(out=cand[:].rearrange("p m d -> p (m d)"), in_=live["ps_s", j][:], func=ACT.Tanh)
+            nc.scalar.activation(out=cand[:].rearrange("p m d -> p (m d)"), in_=live["ps_cand", j][:], func=ACT.Tanh)
 
-        def n_diff(j):
-            diff = keep.tile([P, 2, P], F32, tag="diff")
+        def n_diff(ph, i, j):
+            diff = keep_pool.tile([P, HALVES, P], F32, tag="diff")
             live["diff", j] = diff
-            nc.vector.tensor_sub(out=diff[:], in0=h_nat[:, :, j * P : (j + 1) * P], in1=live["cand", j][:])
+            nc.vector.tensor_sub(out=diff[:], in0=h_cells[:, :, j * P : (j + 1) * P], in1=live["cand", j][:])
 
-        def z_out(j):
-            a_z = epi.tile([P, CELLS], F32, tag="a_z")
-            live["a_z", j] = a_z
-            nc.scalar.copy(out=a_z[:], in_=live["ps_z", j][:])
+        def z_matmuls(ph, i, j):
+            mx_passes("ps_z", ph, i, j, ALL_PASSES, ALL_PASSES)
 
-        def z_gate(j):
-            z = epi.tile([P, 2, P], F32, tag="z")
+        def z_out(ph, i, j):
+            z_in = step_pool.tile([P, CELLS], F32, tag="z_in")
+            live["z_in", j] = z_in
+            nc.scalar.copy(out=z_in[:], in_=live["ps_z", j][:])
+
+        def z_turn(ph, i, j):
+            turn("ps_zc", j, 0, [live["z_in", j]])
+
+        def z_gate(ph, i, j):
+            z = step_pool.tile([P, HALVES, P], F32, tag="z")
             live["z", j] = z
-            nc.scalar.activation(out=z[:].rearrange("p m d -> p (m d)"), in_=live["ps_zn", j][:], func=ACT.Sigmoid)
+            nc.scalar.activation(out=z[:].rearrange("p m d -> p (m d)"), in_=live["ps_zc", j][:], func=ACT.Sigmoid)
 
-        def z_mul(j):
-            gated = epi.tile([P, 2, P], F32, tag="gated")
-            live["gated", j] = gated
+        def z_blend(ph, i, j):
+            gated = step_pool.tile([P, HALVES, P], F32, tag="gated")
             nc.vector.tensor_mul(out=gated[:], in0=live["z", j][:], in1=live["diff", j][:])
+            h_new = step_pool.tile([P, HALVES, P], F32, tag="h_new")
+            live["h_new", j] = h_new
+            nc.vector.tensor_add(out=h_new[:], in0=gated[:], in1=live["cand", j][:])
 
-        def mix_up(j):
-            o_ps = ps_fl.tile([P, CELLS], F32, tag="o_ps")
-            live["o_ps", j] = o_ps
+        def z_mix(ph, i, j):
+            mixed = plain_psum.tile([P, CELLS], F32, tag="mixed")
+            live["mixed", j] = mixed
             nc.tensor.matmul(
-                out=o_ps[:], lhsT=mix[:], rhs=live["cand", j][:].rearrange("p m d -> p (m d)"), start=True, stop=False
-            )
-            nc.tensor.matmul(
-                out=o_ps[:], lhsT=mix[:], rhs=live["gated", j][:].rearrange("p m d -> p (m d)"), start=False, stop=True
+                out=mixed[:], lhsT=mix[:], rhs=live["h_new", j][:].rearrange("p m d -> p (m d)"), start=True, stop=True
             )
 
-        def finish(j):
-            per = STORE // P
-            if j % per == 0:
-                o_sb = outp.tile([P, 2, STORE], F32, tag="o_sb")
-                live["o_sb", j // per] = o_sb
-            o_sb = live["o_sb", j // per]
+        def z_store(ph, i, j):
+            per_store = min(phases[ph][2], SUB) // P
+            first = j - i % per_store
+            if j == first:
+                result = out_pool.tile([P, HALVES, per_store * P], F32, tag="result")
+                live["result", first] = result
+            result = live["result", first]
             nc.scalar.copy(
-                out=o_sb[:, :, (j % per) * P : (j % per + 1) * P],
-                in_=live["o_ps", j][:].rearrange("p (m d) -> p m d", m=2),
+                out=result[:, :, (j - first) * P : (j - first + 1) * P],
+                in_=live["mixed", j][:].rearrange("p (m d) -> p m d", m=HALVES),
             )
-            if j % per == per - 1:
-                lo = (j // per) * STORE
-                nc.scalar.dma_start(out=out[:, lo : lo + STORE].rearrange("(m p) d -> p m d", p=P), in_=o_sb[:])
+            if j == first + per_store - 1:
+                nc.scalar.dma_start(
+                    out=out[:, first * P : (first + per_store) * P].rearrange("(m p) d -> p m d", p=P), in_=result[:]
+                )
 
-        chain = {}
-        bulk = {}
+        steps_of = {
+            GATE_R: (r_matmuls, r_add, r_gate),
+            GATE_N: (n_matmuls, n_out, n_turn, n_tanh, n_diff),
+            GATE_Z: (z_matmuls, z_out, z_turn, z_gate, z_blend, z_mix, z_store),
+        }
 
-        def at(table, slot, fn):
-            if slot not in table:
-                table[slot] = []
-            table[slot].append(fn)
-
-        at(bulk, 3, load_x)
-        at(chain, 4, prep_vectors)
-        for c in range(PASSES):
-            at(chain, 5 + c, lambda c=c: x_transpose(c))
-            at(chain, 6 + c, lambda c=c: x_copy(c))
-            at(chain, 7 + c, lambda c=c: x_quantise(c))
-
-        slot = 0
-        for ph, (gate, d0, width) in enumerate(PHASES):
-            at(bulk, slot, lambda ph=ph, width=width: open_phase(ph, width))
+        phases = []
+        for g0, span in GROUPS:
+            parts = LAST_Z_SPLIT if (g0, span) == GROUPS[-1] else 1
+            phases.append((GATE_R, g0, span, g0, span))
+            phases.append((GATE_N, g0, span, g0, span))
+            for part in range(parts):
+                phases.append((GATE_Z, g0 + part * (span // parts), span // parts, g0, span))
+        copies = []
+        codes_done = []
+        for ph, (gate, d0, width, g0, span) in enumerate(phases):
+            sub = min(SUB, width)
             for c in range(PASSES):
-                pieces = 2 if slot == 0 else 1
-                at(bulk, slot, lambda ph=ph, c=c, gate=gate, d0=d0, width=width, pieces=pieces: load(ph, c, gate, d0, width, pieces))
-                for hh in range(width // SUB):
-                    at(bulk, slot, lambda ph=ph, c=c, hh=hh, slot=slot: regroup(ph, c, hh, slot))
-                    at(bulk, slot + QLAG, lambda ph=ph, c=c, hh=hh, slot=slot: quantise(ph, c, hh, slot))
-                    slot += 1
-            for i in range(width // P):
-                j = d0 // P + i
-                t0 = slot + QLAG + i
-                if gate == GATE_R:
-                    at(chain, t0, lambda j=j, ph=ph, i=i: mx_group("ps_r", j, ph, i, (0, 1, 2, 3, 4)))
-                    at(chain, t0 + 1, lambda j=j: r_add(j))
-                    at(chain, t0 + 2, lambda j=j: r_gate(j))
-                elif gate == GATE_N:
-                    at(chain, t0, lambda j=j, ph=ph, i=i: mx_group("ps_i", j, ph, i, (0,)))
-                    at(chain, t0, lambda j=j, ph=ph, i=i: mx_group("ps_h", j, ph, i, (1, 2, 3, 4)))
-                    at(chain, t0 + 1, lambda j=j: n_out(j))
-                    at(chain, t0 + 2, lambda j=j: flip_group("ps_s", j, DHID, [live["a_i", j], live["v", j]]))
-                    at(chain, t0 + 3, lambda j=j: n_tanh(j))
-                    at(chain, t0 + 4, lambda j=j: n_diff(j))
-                else:
-                    at(chain, t0, lambda j=j, ph=ph, i=i: mx_group("ps_z", j, ph, i, (0, 1, 2, 3, 4)))
-                    at(chain, t0 + 1, lambda j=j: z_out(j))
-                    at(chain, t0 + 2, lambda j=j: flip_group("ps_zn", j, 0, [live["a_z", j]]))
-                    at(chain, t0 + 3, lambda j=j: z_gate(j))
-                    at(chain, t0 + 4, lambda j=j: z_mul(j))
-                    at(chain, t0 + 5, lambda j=j: mix_up(j))
-                    at(chain, t0 + 6, lambda j=j: finish(j))
+                for lo in range(0, width, sub):
+                    copies.append((ph, c, lo, sub))
+            codes_done.append(len(copies) + QUANTISE_LAG)
+        last_phase = len(phases) - 1
 
-        for s in range(slot + 32):
-            for fn in chain.get(s, []):
-                fn()
-            for fn in bulk.get(s, []):
-                fn()
+        for slot in range(len(copies) + DRAIN_SLOTS):
+            for ph, (gate, d0, width, g0, span) in enumerate(phases):
+                steps = steps_of[gate]
+                for k in reversed(range(len(steps))):
+                    i = slot - codes_done[ph] - k
+                    if 0 <= i < width // P and not (ph == last_phase and k == 0):
+                        steps[k](ph, i, d0 // P + i)
+            if slot == VECTORS_SLOT:
+                turn_vectors()
+            for k, step in reversed(list(enumerate((x_transpose, x_copy, x_quantise)))):
+                if 0 <= slot - X_SLOT - k < PASSES:
+                    step(slot - X_SLOT - k)
+            if slot - QUANTISE_LAG - 1 >= 0 and slot - QUANTISE_LAG - 1 < len(copies):
+                ph, c, lo, sub = copies[slot - QUANTISE_LAG - 1]
+                if ph == last_phase:
+                    for i in range(phases[ph][2] // P):
+                        mx_passes("ps_z", ph, i, phases[ph][1] // P + i, ALL_PASSES, (c,))
+            if slot < len(copies):
+                ph, c, lo, sub = copies[slot]
+                gate, d0, width, g0, span = phases[ph]
+                if c == 0 and lo == 0:
+                    open_phase(ph, width)
+                if d0 == g0 and lo == 0:
+                    load_weights(gate, g0, span, c)
+                regroup(slot, live["raw", gate, g0, c], d0 - g0 + lo, sub)
+            if slot == X_LOAD_SLOT:
+                load_x()
+            if 0 <= slot - QUANTISE_LAG < len(copies):
+                ph, c, lo, sub = copies[slot - QUANTISE_LAG]
+                quantise(slot - QUANTISE_LAG, ph, c, lo, sub)

@@ -257,12 +257,15 @@ def tile_fractalengine_pb_kernel(tc, eng_out, tension, hiddens, w_ih, b_ih, w_hh
             live["z", j] = z
             nc.scalar.activation(out=z[:].rearrange("p m d -> p (m d)"), in_=live["ps_zc", j][:], func=ACT.Sigmoid)
 
-        def z_blend(ph, i, j):
+        def z_times(ph, i, j):
             gated = step_pool.tile([P, HALVES, P], F32, tag="gated")
+            live["gated", j] = gated
             nc.vector.tensor_mul(out=gated[:], in0=live["z", j][:], in1=live["diff", j][:])
+
+        def z_plus(ph, i, j):
             h_new = step_pool.tile([P, HALVES, P], F32, tag="h_new")
             live["h_new", j] = h_new
-            nc.vector.tensor_add(out=h_new[:], in0=gated[:], in1=live["cand", j][:])
+            nc.vector.tensor_add(out=h_new[:], in0=live["gated", j][:], in1=live["cand", j][:])
 
         def z_mix(ph, i, j):
             mixed = plain_psum.tile([P, CELLS], F32, tag="mixed")
@@ -290,7 +293,7 @@ def tile_fractalengine_pb_kernel(tc, eng_out, tension, hiddens, w_ih, b_ih, w_hh
         steps_of = {
             GATE_R: (r_matmuls, r_add, r_gate),
             GATE_N: (n_matmuls, n_out, n_turn, n_tanh, n_diff),
-            GATE_Z: (z_matmuls, z_out, z_turn, z_gate, z_blend, z_mix, z_store),
+            GATE_Z: (z_matmuls, z_out, z_turn, z_gate, z_times, z_plus, z_mix, z_store),
         }
 
         phases = []

@@ -92,6 +92,11 @@ def tile_fractalengine_pb_kernel(tc, eng_out, tension, hiddens, w_ih, b_ih, w_hh
             out=mix[:], in0=same_faction[:], scalar=SYNC / FACTION, in1=own[:], op0=ALU.mult, op1=ALU.add
         )
 
+        warm_in = const.tile([P, 1], F32)
+        nc.vector.memset(warm_in[:], 0.0)
+        warm_out = const.tile([P, 1], F32)
+        nc.scalar.activation(out=warm_out[:], in_=warm_in[:], func=ACT.Sigmoid)
+
         vec = const.tile([P, 4 * blocks_all], F32)
         bias_r = const.tile([P, blocks_all], F32)
 

@@ -41,7 +41,6 @@ DRAIN_SLOTS = 16
 def tile_fractalengine_pb_kernel(tc, eng_out, tension, hiddens, w_ih, b_ih, w_hh, b_hh, out):
     nc = tc.nc
     with ExitStack() as ctx:
-        ctx.enter_context(tc.manual_schedule())
         const = ctx.enter_context(tc.tile_pool(name="const", bufs=1))
         raw_pool = ctx.enter_context(tc.tile_pool(name="raw_pool", bufs=PASSES))
         grouped_pool = ctx.enter_context(tc.tile_pool(name="grouped_pool", bufs=QUANTISE_LAG + 3))

@@ -307,43 +307,30 @@ def tile_fractalengine_pb_kernel(tc, eng_out, tension, hiddens, w_ih, b_ih, w_hh
             phases.append((GATE_N, g0, span, g0, span))
             for part in range(parts):
                 phases.append((GATE_Z, g0 + part * (span // parts), span // parts, g0, span))
-        copies = []
-        codes_done = []
-        for ph, (gate, d0, width, g0, span) in enumerate(phases):
-            sub = min(SUB, width)
-            for c in range(PASSES):
-                for lo in range(0, width, sub):
-                    copies.append((ph, c, lo, sub))
-            codes_done.append(len(copies) + QUANTISE_LAG)
         last_phase = len(phases) - 1
 
-        for slot in range(len(copies) + DRAIN_SLOTS):
-            for ph, (gate, d0, width, g0, span) in enumerate(phases):
-                steps = steps_of[gate]
-                for k in reversed(range(len(steps))):
-                    i = slot - codes_done[ph] - k
-                    if 0 <= i < width // P and not (ph == last_phase and k == 0):
-                        steps[k](ph, i, d0 // P + i)
-            if slot == VECTORS_SLOT:
-                turn_vectors()
-            for k, step in reversed(list(enumerate((x_transpose, x_copy, x_quantise)))):
-                if 0 <= slot - X_SLOT - k < PASSES:
-                    step(slot - X_SLOT - k)
-            if slot - QUANTISE_LAG - 1 >= 0 and slot - QUANTISE_LAG - 1 < len(copies):
-                ph, c, lo, sub = copies[slot - QUANTISE_LAG - 1]
-                if ph == last_phase:
-                    for i in range(phases[ph][2] // P):
-                        mx_passes("ps_z", ph, i, phases[ph][1] // P + i, ALL_PASSES, (c,))
-            if slot < len(copies):
-                ph, c, lo, sub = copies[slot]
-                gate, d0, width, g0, span = phases[ph]
-                if c == 0 and lo == 0:
-                    open_phase(ph, width)
-                if d0 == g0 and lo == 0:
+        copy_no = 0
+        for ph, (gate, d0, width, g0, span) in enumerate(phases):
+            open_phase(ph, width)
+            sub = min(SUB, width)
+            for c in range(PASSES):
+                if d0 == g0:
                     load_weights(gate, g0, span, c)
-                regroup(slot, live["raw", gate, g0, c], d0 - g0 + lo, sub)
-            if slot == X_LOAD_SLOT:
-                load_x()
-            if 0 <= slot - QUANTISE_LAG < len(copies):
-                ph, c, lo, sub = copies[slot - QUANTISE_LAG]
-                quantise(slot - QUANTISE_LAG, ph, c, lo, sub)
+                if ph == 0 and c == 1:
+                    load_x()
+                for lo in range(0, width, sub):
+                    regroup(copy_no, live["raw", gate, g0, c], d0 - g0 + lo, sub)
+                    quantise(copy_no, ph, c, lo, sub)
+                    copy_no += 1
+                if ph == last_phase:
+                    for i in range(width // P):
+                        mx_passes("ps_z", ph, i, d0 // P + i, ALL_PASSES, (c,))
+            if ph == 0:
+                for c in range(PASSES):
+                    x_transpose(c)
+                    x_copy(c)
+                    x_quantise(c)
+                turn_vectors()
+            for i in range(width // P):
+                for step in steps_of[gate][1 if ph == last_phase else 0 :]:
+                    step(ph, i, d0 // P + i)

@@ -159,10 +159,7 @@ def tile_fractalengine_pb_kernel(tc, eng_out, tension, hiddens, w_ih, b_ih, w_hh
             live["grouped", slot] = grouped
             dst = grouped[:].rearrange("p (a i) t -> p a t i", i=4)
             src = raw[:, :, lo : lo + sub].rearrange("p t (a i) -> p a t i", i=4)
-            if slot % 2 == 0:
-                nc.vector.tensor_copy(out=dst, in_=src)
-            else:
-                nc.scalar.copy(out=dst, in_=src)
+            nc.any.tensor_copy(out=dst, in_=src)
 
         def quantise(slot, ph, c, lo, sub):
             nc.vector.quantize_mx(

from contextlib import ExitStack

import concourse.mybir as mybir
from concourse.masks import make_identity

FP8X4 = mybir.dt.float8_e4m3fn_x4
BF16 = mybir.dt.bfloat16
F32 = mybir.dt.float32
U32 = mybir.dt.uint32
U8 = mybir.dt.uint8
I32 = mybir.dt.int32
ALU = mybir.AluOpType
ACT = mybir.ActivationFunctionType

P = 128
PACK = 4
K_PASS = P * PACK
CELLS = 256
HALVES = CELLS // P
DOUT = 512
DHID = 2048
PASSES = (DOUT + DHID) // K_PASS
ALL_PASSES = tuple(range(PASSES))
SYNC = 0.15
FACTION = 32
GATE_R, GATE_Z, GATE_N = 0, 1, 2

FLOPS = 2 * CELLS * (DOUT + DHID) * 3 * DHID

GROUPS = ((0, 1024), (1024, 512), (1536, 512))
LAST_Z_SPLIT = 2
SUB = 512

QUANTISE_LAG = 2
X_LOAD_SLOT = 3
X_SLOT = 5
VECTORS_SLOT = 10
DRAIN_SLOTS = 16


def tile_fractalengine_pb_kernel(tc, eng_out, tension, hiddens, w_ih, b_ih, w_hh, b_hh, out):
    nc = tc.nc
    with ExitStack() as ctx:
        const = ctx.enter_context(tc.tile_pool(name="const", bufs=1))
        raw_pool = ctx.enter_context(tc.tile_pool(name="raw_pool", bufs=PASSES))
        grouped_pool = ctx.enter_context(tc.tile_pool(name="grouped_pool", bufs=QUANTISE_LAG + 3))
        x_pool = ctx.enter_context(tc.tile_pool(name="x_pool", bufs=2))
        code_pool = ctx.enter_context(tc.tile_pool(name="code_pool", bufs=3))
        keep_pool = ctx.enter_context(tc.tile_pool(name="keep_pool", bufs=max(group[1] for group in GROUPS) // P))
        step_pool = ctx.enter_context(tc.tile_pool(name="step_pool", bufs=3))
        out_pool = ctx.enter_context(tc.tile_pool(name="out_pool", bufs=2))
        mx_psum = ctx.enter_context(tc.psum_pool(name="mx_psum", bufs=4))
        plain_psum = ctx.enter_context(tc.psum_pool(name="plain_psum", bufs=2))

        ident = const.tile([P, P], F32)
        make_identity(nc, ident[:])
        ident_bf = const.tile([P, P], BF16)
        make_identity(nc, ident_bf[:])

        blocks_all = DHID // P
        vec_rows = const.tile([P, P], BF16)
        nc.vector.memset(vec_rows[:].bitcast(I32), 0)
        lift = const.tile([P, CELLS], BF16)
        nc.vector.memset(lift[:].bitcast(I32), 0)
        nc.vector.memset(lift[32:64, :], 1.0)
        nc.vector.memset(lift[64:96, :], 1.0)
        rows = const.tile([P, 2 * DHID], BF16)
        nc.vector.memset(rows[:].bitcast(I32), 0)
        tension_all = const.tile([P, CELLS], BF16)

        last_row = w_ih[DOUT : DOUT + 1, :]
        nc.gpsimd.dma_start(out=vec_rows[0:16, :], in_=last_row[:, 0:DHID].rearrange("o (r c) -> (o r) c", c=P))
        nc.gpsimd.dma_start(out=vec_rows[16:32, :], in_=b_ih[0:DHID].rearrange("(r c) -> r c", c=P))
        nc.gpsimd.dma_start(out=vec_rows[32:48, :], in_=b_hh[0:DHID].rearrange("(r c) -> r c", c=P))
        nc.gpsimd.dma_start(out=vec_rows[48:64, :], in_=b_hh[2 * DHID : 3 * DHID].rearrange("(r c) -> r c", c=P))
        nc.gpsimd.dma_start(out=tension_all[:], in_=tension.partition_broadcast(P))
        nc.gpsimd.dma_start(out=lift[0:1, :], in_=tension.rearrange("(o n) -> o n", o=1))
        nc.gpsimd.dma_start(out=rows[0:1, :], in_=last_row[:, DHID : 3 * DHID])
        nc.gpsimd.dma_start(out=rows[32:33, :], in_=b_ih[DHID : 3 * DHID].rearrange("(o n) -> o n", o=1))
        nc.gpsimd.dma_start(out=rows[64:65, 0:DHID], in_=b_hh[DHID : 2 * DHID].rearrange("(o n) -> o n", o=1))

        same_faction = const.tile([P, P], F32)
        nc.vector.memset(same_faction[:], 0.0)
        for f in range(P // FACTION):
            members = slice(f * FACTION, (f + 1) * FACTION)
            nc.vector.memset(same_faction[members, members], 1.0)
        own = const.tile([P, P], F32)
        nc.vector.tensor_scalar_mul(out=own[:], in0=ident[:], scalar1=1.0 - SYNC)
        mix = const.tile([P, P], F32)
        nc.vector.scalar_tensor_tensor(
            out=mix[:], in0=same_faction[:], scalar=SYNC / FACTION, in1=own[:], op0=ALU.mult, op1=ALU.add
        )

        warm_in = const.tile([P, 1], F32)
        nc.vector.memset(warm_in[:], 0.0)
        warm_out = const.tile([P, 1], F32)
        nc.scalar.activation(out=warm_out[:], in_=warm_in[:], func=ACT.Sigmoid)

        vec = const.tile([P, 4 * blocks_all], F32)
        bias_r = const.tile([P, blocks_all], F32)

        def turn_vectors():
            turned = plain_psum.tile([P, P], BF16, tag="turned")
            nc.tensor.transpose(turned[:], vec_rows[:], ident_bf[:])
            nc.vector.tensor_copy(out=vec[:], in_=turned[:, 0 : 4 * blocks_all])
            nc.vector.tensor_add(
                out=bias_r[:], in0=vec[:, blocks_all : 2 * blocks_all], in1=vec[:, 2 * blocks_all : 3 * blocks_all]
            )

        live = {}

        h_cells = const.tile([P, HALVES, DHID], BF16)
        e_cells = const.tile([P, HALVES, DOUT], BF16)
        x_codes = const.tile([P, PASSES, CELLS], U32, align_bytes=64)
        x_scales = const.tile([P, PASSES, CELLS], U8, align_bytes=64)

        def load_x():
            nc.sync.dma_start(out=e_cells[:], in_=eng_out.rearrange("(m p) k -> p m k", p=P))
            nc.sync.dma_start(out=h_cells[:], in_=hiddens.rearrange("(m p) k -> p m k", p=P))

        def x_transpose(c):
            words = (e_cells if c == 0 else h_cells)[:].bitcast(F32)
            base = 0 if c == 0 else (c - 1) * (K_PASS // 2)
            planes = mx_psum.tile([P, 2, CELLS], F32, tag="mx")
            live["x_planes", c] = planes
            for u in range(2):
                for m in range(HALVES):
                    nc.tensor.transpose(
                        planes[:, u, m * P : (m + 1) * P], words[:, m, base + u : base + K_PASS // 2 : 2], ident[:]
                    )

        def x_copy(c):
            x_grouped = x_pool.tile([P, CELLS, PACK], BF16, align_bytes=64, tag="x_grouped")
            live["x_grouped", c] = x_grouped
            nc.scalar.copy(out=x_grouped[:].bitcast(F32), in_=live["x_planes", c][:].rearrange("p u n -> p n u"))

        def x_quantise(c):
            nc.vector.quantize_mx(
                out=x_codes[:, c, :].bitcast(FP8X4),
                scales=x_scales[:, c, :],
                in_=live["x_grouped", c][:].rearrange("p n t -> p (n t)"),
            )

        def load_weights(gate, g0, span, c):
            raw = raw_pool.tile([P, PACK, span], BF16, tag="raw")
            live["raw", gate, g0, c] = raw
            cols = slice(gate * DHID + g0, gate * DHID + g0 + span)
            src = w_ih[0:K_PASS, cols] if c == 0 else w_hh[(c - 1) * K_PASS : c * K_PASS, cols]
            nc.sync.dma_start(out=raw[:], in_=src.rearrange("(p t) w -> p t w", t=PACK))

        def open_phase(ph, width):
            codes = code_pool.tile([P, PASSES, width], U32, align_bytes=64, tag="codes")
            scales = code_pool.tile([P, PASSES, width], U8, align_bytes=64, tag="scales")
            live["codes", ph] = codes
            live["scales", ph] = scales

        def regroup(slot, raw, lo, sub):
            grouped = grouped_pool.tile([P, sub, PACK], BF16, align_bytes=64, tag="grouped")
            live["grouped", slot] = grouped
            dst = grouped[:].rearrange("p (a i) t -> p a t i", i=4)
            src = raw[:, :, lo : lo + sub].rearrange("p t (a i) -> p a t i", i=4)
            nc.any.tensor_copy(out=dst, in_=src)

        def quantise(slot, ph, c, lo, sub):
            nc.vector.quantize_mx(
                out=live["codes", ph][:, c, lo : lo + sub].bitcast(FP8X4),
                scales=live["scales", ph][:, c, lo : lo + sub],
                in_=live["grouped", slot][:].rearrange("p w t -> p (w t)"),
            )

        def mx_passes(name, ph, i, j, group, passes):
            if passes[0] == group[0]:
                acc = mx_psum.tile([P, CELLS], F32, tag="mx")
                live[name, j] = acc
            for c in passes:
                nc.tensor.matmul_mx(
                    out=live[name, j][:],
                    lhsT=live["codes", ph][:, c, i * P : (i + 1) * P].bitcast(FP8X4),
                    lhsT_scale=live["scales", ph][:, c, i * P : (i + 1) * P],
                    rhs=x_codes[:, c, :].bitcast(FP8X4),
                    rhs_scale=x_scales[:, c, :],
                    start=(c == group[0]),
                    stop=(c == group[-1]),
                )

        def turn(name, j, row0, parts):
            acc = plain_psum.tile([P, CELLS], F32, tag="turned")
            live[name, j] = acc
            for m in range(HALVES):
                half = slice(m * P, (m + 1) * P)
                nc.tensor.matmul(
                    out=acc[:, half], lhsT=lift[:, half], rhs=rows[:, row0 + j * P : row0 + (j + 1) * P],
                    start=True, stop=False,
                )
                for part in parts:
                    nc.tensor.matmul(
                        out=acc[:, half], lhsT=part[:, half], rhs=ident[:], is_transpose=True,
                        start=False, stop=(part is parts[-1]),
                    )

        def r_matmuls(ph, i, j):
            mx_passes("ps_r", ph, i, j, ALL_PASSES, ALL_PASSES)

        def r_add(ph, i, j):
            r_in = step_pool.tile([P, CELLS], F32, tag="r_in")
            live["r_in", j] = r_in
            nc.vector.scalar_tensor_tensor(
                out=r_in[:], in0=tension_all[:], scalar=vec[:, j : j + 1], in1=live["ps_r", j][:],
                op0=ALU.mult, op1=ALU.add,
            )

        def r_gate(ph, i, j):
            r = keep_pool.tile([P, CELLS], F32, tag="r")
            live["r", j] = r
            nc.scalar.activation(out=r[:], in_=live["r_in", j][:], func=ACT.Sigmoid, bias=bias_r[:, j : j + 1], scale=1.0)

        def n_matmuls(ph, i, j):
            mx_passes("ps_inn", ph, i, j, ALL_PASSES[:1], ALL_PASSES[:1])
            mx_passes("ps_hn", ph, i, j, ALL_PASSES[1:], ALL_PASSES[1:])

        def n_out(ph, i, j):
            inn = step_pool.tile([P, CELLS], F32, tag="inn")
            live["inn", j] = inn
            nc.scalar.copy(out=inn[:], in_=live["ps_inn", j][:])
            r_hn = step_pool.tile([P, CELLS], F32, tag="r_hn")
            live["r_hn", j] = r_hn
            nc.vector.scalar_tensor_tensor(
                out=r_hn[:], in0=live["ps_hn", j][:], scalar=vec[:, 3 * blocks_all + j : 3 * blocks_all + j + 1],
                in1=live["r", j][:], op0=ALU.add, op1=ALU.mult,
            )

        def n_turn(ph, i, j):
            turn("ps_cand", j, DHID, [live["inn", j], live["r_hn", j]])

        def n_tanh(ph, i, j):
            cand = keep_pool.tile([P, HALVES, P], F32, tag="cand")
            live["cand", j] = cand
            nc.scalar.activation(out=cand[:].rearrange("p m d -> p (m d)"), in_=live["ps_cand", j][:], func=ACT.Tanh)

        def n_diff(ph, i, j):
            diff = keep_pool.tile([P, HALVES, P], F32, tag="diff")
            live["diff", j] = diff
            nc.vector.tensor_sub(out=diff[:], in0=h_cells[:, :, j * P : (j + 1) * P], in1=live["cand", j][:])

        def z_matmuls(ph, i, j):
            mx_passes("ps_z", ph, i, j, ALL_PASSES, ALL_PASSES)

        def z_out(ph, i, j):
            z_in = step_pool.tile([P, CELLS], F32, tag="z_in")
            live["z_in", j] = z_in
            nc.scalar.copy(out=z_in[:], in_=live["ps_z", j][:])

        def z_turn(ph, i, j):
            turn("ps_zc", j, 0, [live["z_in", j]])

        def z_gate(ph, i, j):
            z = step_pool.tile([P, HALVES, P], F32, tag="z")
            live["z", j] = z
            nc.scalar.activation(out=z[:].rearrange("p m d -> p (m d)"), in_=live["ps_zc", j][:], func=ACT.Sigmoid)

        def z_times(ph, i, j):
            gated = step_pool.tile([P, HALVES, P], F32, tag="gated")
            live["gated", j] = gated
            nc.vector.tensor_mul(out=gated[:], in0=live["z", j][:], in1=live["diff", j][:])

        def z_plus(ph, i, j):
            h_new = step_pool.tile([P, HALVES, P], F32, tag="h_new")
            live["h_new", j] = h_new
            nc.vector.tensor_add(out=h_new[:], in0=live["gated", j][:], in1=live["cand", j][:])

        def z_mix(ph, i, j):
            mixed = plain_psum.tile([P, CELLS], F32, tag="mixed")
            live["mixed", j] = mixed
            nc.tensor.matmul(
                out=mixed[:], lhsT=mix[:], rhs=live["h_new", j][:].rearrange("p m d -> p (m d)"), start=True, stop=True
            )

        def z_store(ph, i, j):
            per_store = min(phases[ph][2], SUB) // P
            first = j - i % per_store
            if j == first:
                result = out_pool.tile([P, HALVES, per_store * P], F32, tag="result")
                live["result", first] = result
            result = live["result", first]
            nc.scalar.copy(
                out=result[:, :, (j - first) * P : (j - first + 1) * P],
                in_=live["mixed", j][:].rearrange("p (m d) -> p m d", m=HALVES),
            )
            if j == first + per_store - 1:
                nc.scalar.dma_start(
                    out=out[:, first * P : (first + per_store) * P].rearrange("(m p) d -> p m d", p=P), in_=result[:]
                )

        steps_of = {
            GATE_R: (r_matmuls, r_add, r_gate),
            GATE_N: (n_matmuls, n_out, n_turn, n_tanh, n_diff),
            GATE_Z: (z_matmuls, z_out, z_turn, z_gate, z_times, z_plus, z_mix, z_store),
        }

        phases = []
        for g0, span in GROUPS:
            parts = LAST_Z_SPLIT if (g0, span) == GROUPS[-1] else 1
            phases.append((GATE_R, g0, span, g0, span))
            phases.append((GATE_N, g0, span, g0, span))
            for part in range(parts):
                phases.append((GATE_Z, g0 + part * (span // parts), span // parts, g0, span))
        last_phase = len(phases) - 1

        copy_no = 0
        for ph, (gate, d0, width, g0, span) in enumerate(phases):
            open_phase(ph, width)
            sub = min(SUB, width)
            for c in range(PASSES):
                if d0 == g0:
                    load_weights(gate, g0, span, c)
                if ph == 0 and c == 1:
                    load_x()
                for lo in range(0, width, sub):
                    regroup(copy_no, live["raw", gate, g0, c], d0 - g0 + lo, sub)
                    quantise(copy_no, ph, c, lo, sub)
                    copy_no += 1
                if ph == last_phase:
                    for i in range(width // P):
                        mx_passes("ps_z", ph, i, d0 // P + i, ALL_PASSES, (c,))
            if ph == 0:
                for c in range(PASSES):
                    x_transpose(c)
                    x_copy(c)
                    x_quantise(c)
                turn_vectors()
            for i in range(width // P):
                for step in steps_of[gate][1 if ph == last_phase else 0 :]:
                    step(ph, i, d0 // P + i)
